import numpy as np
import ml_dtypes


def mxq(x, axis, fmt="e4m3"):
    dtype, down = {"e4m3": (ml_dtypes.float8_e4m3fn, 7), "e5m2": (ml_dtypes.float8_e5m2, 14)}[fmt]
    v = np.moveaxis(np.asarray(x, np.float32).astype(ml_dtypes.bfloat16).astype(np.float64), axis, -1)
    blocks = v.reshape(v.shape[:-1] + (-1, 32))
    amax = np.abs(blocks).max(-1, keepdims=True)
    byte = np.maximum(np.where(amax > 0, np.frexp(amax)[1] - 1 + 127, 0) - down, 1)
    scale = np.exp2(byte - 127.0)
    codes = (blocks / scale).astype(np.float32).astype(dtype).astype(np.float64)
    return np.moveaxis((codes * scale).reshape(v.shape), -1, axis)


WIDE = False


def mx_kscale(k):
    if not WIDE:
        return np.ones(k)
    levels = np.array([10, -10, 5, -5, 0])
    if k % 512:
        return np.exp2(np.random.permutation(np.resize(levels, k // 32))).repeat(32)
    a = np.empty((k // 512, 16))
    for p in range(k // 512):
        a[p, :8] = np.random.permutation(np.resize(levels, 8))
        for g in range(8):
            far = levels[np.abs(levels - a[p, g]) >= 10]
            a[p, g + 8] = far[np.random.randint(len(far))]
    return np.exp2(a.ravel()).repeat(32)


BF16 = ml_dtypes.bfloat16


def bf(x):
    return np.asarray(x, np.float32).astype(BF16)


def f64(x):
    return np.asarray(x).astype(np.float64)


B, T, C, H, KH, D = 4, 128, 2048, 16, 4, 128
HD = H * D


def sigmoid(v):
    return 1.0 / (1.0 + np.exp(-v))


def setup_inputs():
    s, t = mx_kscale(C), mx_kscale(HD)
    return {"x": bf(np.random.standard_normal((B, T, C)) * s),
            "y_attn": bf((np.random.standard_normal((B, T, HD)) * 0.3 * t).reshape(B, T, H, D)),
            "w_gate": bf(np.random.standard_normal((C, HD)) / np.sqrt(C) / s[:, None]),
            "w_proj": bf(np.random.standard_normal((HD, C)) * 3.0 / np.sqrt(HD) / t[:, None])}


def reference(x, y_attn, w_gate, w_proj):
    gate = sigmoid((mxq(f64(x), 2, "e4m3") @ mxq(f64(w_gate), 0, "e4m3")).reshape(B, T, H, D))
    y = f64(y_attn) * gate
    return mxq(y.reshape(B, T, HD), 2, "e4m3") @ mxq(f64(w_proj), 0, "e4m3")

@@ -1,0 +1,381 @@
+from contextlib import ExitStack
+
+import concourse.mybir as mybir
+from concourse.masks import make_identity
+
+F32 = mybir.dt.float32
+BF16 = mybir.dt.bfloat16
+U32 = mybir.dt.uint32
+U8 = mybir.dt.uint8
+FP8X4 = mybir.dt.float8_e4m3fn_x4
+ACT = mybir.ActivationFunctionType
+ALU = mybir.AluOpType
+
+P = 128
+M = 512
+C = 2048
+NG = 4
+CH = 512
+MT = M // P
+
+FLOPS = 2 * 2 * M * C * C
+
+GATE_LOADS = ((0, 512), (512, 512), (1024, 1024))
+PROJ_LOADS = ((0, 1024), (1024, 1024))
+PROJ_CHUNKS = (((0, 512), (512, 512)), ((1024, 512), (1536, 256), (1792, 256)))
+GATE_K_FIRST = (False,False,True)
+PROJ_K_FIRST = (0, 0)
+
+Y_AFTER = (4, 10)
+RAW_KIB = 96
+
+V_NONE, V_S_JOB, V_V_JOB = 256, 416, 96
+LAG_SIG = 2
+LAG_MUL = 3
+LAG_HQ = 0
+LAG_OUT = 4
+LAST_V = (1, 3)
+
+NSLOT = 5
+NB_C = 12
+X_ON_V = ()
+SIG_GAP = 0
+MUL_GAP = 0
+OUT_GAP = 1
+V_STEP = 192
+V_FIRST = {}
+X_GAP = 1
+NB_GRP = 4
+NB_OUT = 8
+X_LOAD = (1, 2)
+X_STEP = (0,1)
+X_FIRST = 1
+X_S = 1.5
+OUT_V = ()
+Y0 = 4
+V_NONE = 256
+
+
+def tile_multiheadattention_pb_kernel(tc, x, y_attn, w_gate, w_proj, out):
+    nc = tc.nc
+    xf = x.flatten_outer_dims()
+    yf = y_attn.rearrange("b t h d -> (b t) (h d)")
+    of = out.flatten_outer_dims()
+
+    with ExitStack() as ctx:
+        const = ctx.enter_context(tc.tile_pool(name="const", bufs=1))
+        keep = ctx.enter_context(tc.tile_pool(name="keep", bufs=1))
+        rawp = ctx.enter_context(tc.tile_pool(name="raw", bufs=NSLOT))
+        grpp = ctx.enter_context(tc.tile_pool(name="grpp", bufs=NB_GRP))
+        xgp = ctx.enter_context(tc.tile_pool(name="xgp", bufs=4))
+        wcp = ctx.enter_context(tc.tile_pool(name="wcp", bufs=NB_C))
+        sigp = ctx.enter_context(tc.tile_pool(name="sigp", bufs=2))
+        hgp = ctx.enter_context(tc.tile_pool(name="hgp", bufs=2))
+        outp = ctx.enter_context(tc.tile_pool(name="outp", bufs=NB_OUT))
+        warmp = ctx.enter_context(tc.tile_pool(name="warmp", bufs=1))
+        psum = ctx.enter_context(tc.psum_pool(name="psum", bufs=6))
+        psy = ctx.enter_context(tc.psum_pool(name="psy", bufs=2))
+
+        ctx.enter_context(tc.manual_schedule())
+
+        warm_in = warmp.tile([P, 1], F32, name="warm_in")
+        warm_out = warmp.tile([P, 1], F32, name="warm_out")
+        nc.vector.memset(warm_in[:], 0.0)
+        nc.scalar.activation(out=warm_out[:], in_=warm_in[:], func=ACT.Sigmoid)
+
+        ident = const.tile([P, P], F32, name="ident")
+        make_identity(nc, ident[:])
+
+        x_sb = [keep.tile([P, C], BF16, name="x_sb%d" % mt) for mt in range(MT)]
+        y_sb = [keep.tile([P, MT, 1024], BF16, name="y_sb%d" % h) for h in range(2)]
+        xc = keep.tile([P, NG, M], U32, name="xc", align_bytes=64)
+        xs = keep.tile([P, NG, M], U8, name="xs", align_bytes=64)
+        hc = keep.tile([P, NG, M], U32, name="hc", align_bytes=64)
+        hs = keep.tile([P, NG, M], U8, name="hs", align_bytes=64)
+
+        steps = []
+        plan = []
+        chunks = []
+        for stage, loads, kfirst in (("g", GATE_LOADS, GATE_K_FIRST), ("p", PROJ_LOADS, PROJ_K_FIRST)):
+            for b, (c0, w) in enumerate(loads):
+                parts = [(c, CH) for c in range(c0, c0 + w, CH)] if stage == "g" else PROJ_CHUNKS[b]
+                n0 = len(chunks)
+                chunks += [(stage, lo, pw) for lo, pw in parts]
+                nk = len(parts) if kfirst[b] is True else int(kfirst[b])
+                order = [(g, i) for g in range(NG) for i in range(nk)]
+                order += [(g, i) for i in range(nk, len(parts)) for g in range(NG)]
+                for g in range(NG):
+                    plan.append((stage, c0, w, g))
+                for g, i in order:
+                    steps.append((stage, (stage, c0, g), parts[i][0] - c0, parts[i][1], g, n0 + i))
+        NGC = sum(1 for ch in chunks if ch[0] == "g")
+        NI = len(steps)
+
+        raws = {}
+        left = {}
+
+        loads = []
+        for n, pl in enumerate(plan):
+            loads.append(("w",) + pl)
+            for h in range(2):
+                if n + 1 == X_LOAD[h]:
+                    loads += [("x", 2 * h), ("x", 2 * h + 1)]
+            for h in range(2):
+                if n + 1 == Y_AFTER[h]:
+                    loads.append(("y", h))
+        room = [NSLOT]
+        slots = {}
+
+        def load_more():
+            while loads:
+                ld = loads[0]
+                if ld[0] == "x":
+                    nc.sync.dma_start(out=x_sb[ld[1]][:], in_=xf[P * ld[1]:P * (ld[1] + 1), :])
+                elif ld[0] == "y":
+                    nc.sync.dma_start(
+                        out=y_sb[ld[1]][:],
+                        in_=yf[:, 1024 * ld[1]:1024 * (ld[1] + 1)].rearrange("(t p) c -> p t c", p=P),
+                    )
+                else:
+                    stage, c0, w, g = ld[1:]
+                    n = 2048 // w
+                    sk = (stage, c0, g // n)
+                    if sk not in slots:
+                        if room[0] == 0:
+                            return
+                        room[0] -= 1
+                        slots[sk] = rawp.tile([P, n, 4, w], BF16, name="raw")
+                        left[sk] = n * w
+                    raw = slots[sk][:, g % n, :, :]
+                    raws[(stage, c0, g)] = (raw, sk)
+                    src = (w_gate if stage == "g" else w_proj)[512 * g:512 * (g + 1), c0:c0 + w]
+                    nc.sync.dma_start(out=raw, in_=src.rearrange("(p j) c -> p j c", j=4))
+                loads.pop(0)
+
+        load_more()
+
+        grps = {}
+        cods = {}
+
+        def regroup(k, cv):
+            stage, key, c0, w, g, ch = steps[k]
+            grp = grpp.tile([P, 4 * w], BF16, name="grp", align_bytes=64)
+            grps[k] = grp
+            raw, sk = raws[key]
+            for eng, a, b in (("v", 0, cv), ("s", cv, w)):
+                if b > a:
+                    if stage == "g":
+                        dst = grp[:].rearrange("p (t b m j) -> p b j m t", t=4, m=2, j=4)[:, a // 8:b // 8]
+                        src = raw[:, :, c0 + a:c0 + b].rearrange("p j (b m t) -> p b j m t", m=2, t=4)
+                    else:
+                        dst = grp[:, 4 * a:4 * b].rearrange("p (c i t) -> p c t i", i=8, t=4)
+                        src = raw[:, :, c0 + a:c0 + b].rearrange("p t (c i) -> p c t i", i=8)
+                    if eng == "v":
+                        nc.vector.tensor_copy(out=dst, in_=src)
+                    else:
+                        nc.scalar.copy(out=dst, in_=src)
+            left[sk] -= w
+            if left[sk] == 0:
+                room[0] += 1
+            load_more()
+
+        def x_transposes(half):
+            xgs = []
+            for g in range(NG):
+                ps = psum.tile([P, 2, 256], F32, name="bank")
+                for u in range(2):
+                    for i in range(2):
+                        nc.tensor.transpose(
+                            ps[:, u, P * i:P * (i + 1)],
+                            x_sb[2 * half + i][:].bitcast(F32)[:, 256 * g + u:256 * (g + 1):2],
+                            ident[:],
+                        )
+                xg = xgp.tile([P, 1024], BF16, name="xg", align_bytes=64)
+                xgs.append(xg)
+                dst = xg[:].bitcast(F32).rearrange("p (m u) -> p m u", u=2)
+                src = ps[:].rearrange("p u m -> p m u")
+                if g in X_ON_V:
+                    nc.vector.tensor_copy(out=dst, in_=src)
+                else:
+                    nc.scalar.copy(out=dst, in_=src)
+            return xgs
+
+        def x_quantise(half, xgs):
+            for g in range(NG):
+                nc.vector.quantize_mx(
+                    out=xc[:, g, 256 * half:256 * (half + 1)].bitcast(FP8X4),
+                    scales=xs[:, g, 256 * half:256 * (half + 1)],
+                    in_=xgs[g][:],
+                )
+
+        banks = {}
+        queue = [(ch, g) for ch in range(len(chunks)) for g in range(NG)]
+        done = set()
+        todo = {}
+
+        def later(k, what):
+            todo.setdefault(k, []).append(what)
+
+        def passes(ch, g):
+            stage, lo, w = chunks[ch]
+            wcod, wsca = cods[(ch, g)]
+            for b in range(4):
+                if g == 0 and stage == "p" and b == 3:
+                    banks[(ch, b)] = psy.tile([P, w], F32, name="ybank")
+                elif g == 0:
+                    banks[(ch, b)] = psum.tile([P, M if stage == "g" else w], F32, name="bank")
+                if stage == "g":
+                    nc.tensor.matmul_mx(
+                        out=banks[(ch, b)][:],
+                        lhsT=wcod[:, P * b:P * (b + 1)].bitcast(FP8X4),
+                        lhsT_scale=wsca[:, P * b:P * (b + 1)],
+                        rhs=xc[:, g, :].bitcast(FP8X4),
+                        rhs_scale=xs[:, g, :],
+                        start=(g == 0),
+                        stop=(g == NG - 1),
+                    )
+                else:
+                    nc.tensor.matmul_mx(
+                        out=banks[(ch, b)][:],
+                        lhsT=hc[:, g, P * b:P * (b + 1)].bitcast(FP8X4),
+                        lhsT_scale=hs[:, g, P * b:P * (b + 1)],
+                        rhs=wcod[:].bitcast(FP8X4),
+                        rhs_scale=wsca[:],
+                        start=(g == 0),
+                        stop=(g == NG - 1),
+                    )
+
+        def ready(ch, g):
+            if (ch, g) not in cods or "x" not in done:
+                return False
+            if ch >= NGC and ("hq", g) not in done:
+                return False
+            if g == 0 and ch > 0:
+                if ch == NGC:
+                    return ("sig", NGC - 1) in done and ("mul", NGC - 1) in done
+                if ch < NGC:
+                    return ("sig", ch - 1) in done
+                if ch >= NGC + 2:
+                    return ("out", ch - 2) in done
+            return True
+
+        def flush(now):
+            while queue and ready(*queue[0]):
+                ch, g = queue.pop(0)
+                passes(ch, g)
+                if g == NG - 1:
+                    if ch < NGC:
+                        later(now + LAG_SIG, ("sig", ch, 0))
+                        later(now + LAG_SIG + SIG_GAP, ("sig", ch, 1))
+                        later(now + LAG_MUL, ("mul", ch, 0))
+                        later(now + LAG_MUL + MUL_GAP, ("mul", ch, 1))
+                        later(now + LAG_MUL + MUL_GAP + LAG_HQ, ("hq", ch, 0))
+                        if ch + 1 < NGC:
+                            later(now + LAG_MUL + MUL_GAP + 1, ("ytr", ch + 1, 0))
+                    else:
+                        later(now + LAG_OUT, ("out", ch, 0))
+                        later(now + LAG_OUT + OUT_GAP, ("out", ch, 1))
+
+        def quantise(k, now):
+            stage, key, c0, w, g, ch = steps[k]
+            wcod = wcp.tile([P, w], U32, name="wcod", align_bytes=64)
+            wsca = wcp.tile([P, w], U8, name="wsca", align_bytes=64)
+            cods[(ch, g)] = (wcod, wsca)
+            nc.vector.quantize_mx(out=wcod[:].bitcast(FP8X4), scales=wsca[:], in_=grps[k][:])
+            flush(now)
+
+        sigs = {}
+        yps = {}
+        hgs = {}
+
+        def run_job(job, now):
+            kind, ch, part = job
+            if kind == "sig":
+                if part == 0:
+                    sigs[ch] = sigp.tile([P, 4, M], F32, name="sig")
+                for j in (2 * part, 2 * part + 1):
+                    nc.scalar.activation(out=sigs[ch][:, j, :], in_=banks[(ch, j)][:], func=ACT.Sigmoid)
+                if part == 1:
+                    done.add(("sig", ch))
+                    flush(now)
+            elif kind == "ytr":
+                yw = y_sb[ch // 2][:, :, CH * (ch % 2):CH * (ch % 2 + 1)]
+                for half in range(2):
+                    yp = psy.tile([P, 2, 256], F32, name="ybank")
+                    yps[(ch, half)] = yp
+                    for u in range(2):
+                        for i in range(2):
+                            nc.tensor.transpose(
+                                yp[:, u, P * i:P * (i + 1)],
+                                yw[:, 2 * half + i, :].bitcast(F32)[:, u::2],
+                                ident[:],
+                            )
+            elif kind == "mul":
+                if part == 0:
+                    hgs[ch] = hgp.tile([P, 4 * M], BF16, name="hg", align_bytes=64)
+                nc.vector.tensor_tensor(
+                    out=hgs[ch][:, 1024 * part:1024 * (part + 1)].rearrange("p (m u e) -> p m u e", u=2, e=2),
+                    in0=sigs[ch][:, :, 256 * part:256 * (part + 1)].rearrange("p (u e) m -> p m u e", e=2),
+                    in1=yps[(ch, part)][:].bitcast(BF16).rearrange("p u (m e) -> p m u e", e=2),
+                    op=ALU.mult,
+                )
+                if part == 1:
+                    done.add(("mul", ch))
+            elif kind == "hq":
+                nc.vector.quantize_mx(out=hc[:, ch, :].bitcast(FP8X4), scales=hs[:, ch, :], in_=hgs[ch][:])
+                done.add(("hq", ch))
+                flush(now)
+            elif kind == "out":
+                stage, lo, w = chunks[ch]
+                last = ch == len(chunks) - 1
+                for mt in (2 * part, 2 * part + 1):
+                    ob = outp.tile([P, w], F32, name="ob")
+                    if mt in (LAST_V if last else OUT_V):
+                        nc.vector.tensor_copy(out=ob[:], in_=banks[(ch, mt)][:])
+                    else:
+                        nc.scalar.copy(out=ob[:], in_=banks[(ch, mt)][:])
+                    nc.sync.dma_start(out=of[P * mt:P * (mt + 1), lo:lo + w], in_=ob[:])
+                if part == 1:
+                    done.add(("out", ch))
+                    flush(now)
+
+        later(Y0, ("ytr", 0, 0))
+        xgs = {}
+        k = 0
+        while k <= NI or any(n >= k for n in todo):
+            jobs = todo.get(k, [])
+            s_job = sum(1 for j in jobs if j[0] == "sig")
+            s_job += sum(1 for j in jobs if j[0] == "out") * (2 - len(OUT_V)) / 2
+            s_job += sum(1 for h in range(2) if k == X_STEP[h]) * X_S
+            v_job = sum(1 for j in jobs if j[0] == "mul")
+            for job in jobs:
+                if job[0] in ("sig", "out", "ytr", "mul"):
+                    run_job(job, k)
+            for h in range(2):
+                if k == X_STEP[h] and X_FIRST:
+                    xgs[h] = x_transposes(h)
+            if k < NI:
+                w = steps[k][3]
+                cols = int(V_NONE + V_STEP * (s_job - v_job))
+                if k in V_FIRST:
+                    cols = V_FIRST[k]
+                if w < CH:
+                    cols = cols * w // CH
+                cols = min(max(cols // 32 * 32, 0), w)
+                regroup(k, cols)
+            if 0 < k <= NI:
+                quantise(k - 1, k)
+            for h in range(2):
+                if k == X_STEP[h] and not X_FIRST:
+                    xgs[h] = x_transposes(h)
+            for job in todo.get(k, []):
+                if job[0] == "hq":
+                    run_job(job, k)
+            for h in range(2):
+                if k == X_STEP[h] + X_GAP:
+                    x_quantise(h, xgs[h])
+                    if h == 1:
+                        done.add("x")
+                        flush(k)
+            k += 1
+        assert not queue

@@ -20,39 +20,48 @@ MT = M // P
 
 FLOPS = 2 * 2 * M * C * C
 
-GATE_LOADS = ((0, 512), (512, 512), (1024, 1024))
+GATE_LOADS = ((0, 512), (512, 512), (1024, 512), (1536, 512))
 PROJ_LOADS = ((0, 1024), (1024, 1024))
 PROJ_CHUNKS = (((0, 512), (512, 512)), ((1024, 512), (1536, 256), (1792, 256)))
-GATE_K_FIRST = (False,False,True)
+GATE_K_FIRST = (False,)*4
 PROJ_K_FIRST = (0, 0)
 
-Y_AFTER = (4, 10)
+Y_AFTER = (8,11)
 RAW_KIB = 96
 
 V_NONE, V_S_JOB, V_V_JOB = 256, 416, 96
-LAG_SIG = 2
-LAG_MUL = 3
+LAG_SIG = 3
+LAG_MUL = 5
 LAG_HQ = 0
-LAG_OUT = 4
+LAG_OUT = 5
 LAST_V = (1, 3)
 
 NSLOT = 5
 NB_C = 12
 X_ON_V = ()
-SIG_GAP = 0
-MUL_GAP = 0
-OUT_GAP = 1
+SIG_AT = (0,0,0,0)
+MUL_AT = (0,0,0,0)
+OUT_AT = (0,0,0,0)
+MUL_W = 2
+LAG_YTR = 0
+LAG_SIG_L = 2
+LAG_MUL_L = 3
 V_STEP = 192
 V_FIRST = {}
-X_GAP = 1
-NB_GRP = 4
+X_GAP = 0
+WARM0 = 0
+WARM_X = (0,0,0,0)
+WARM_C = (0,)*10
+NB_SIG = 2
+SPLIT = 1
+NB_GRP = 5
 NB_OUT = 8
-X_LOAD = (1, 2)
-X_STEP = (0,1)
+X_LOAD = (1,1,3,3)
+X_STEP = (1,3)
 X_FIRST = 1
-X_S = 1.5
+X_S = 0
 OUT_V = ()
-Y0 = 4
+Y0 = 6
 V_NONE = 256
 
 
@@ -69,7 +78,7 @@ def tile_multiheadattention_pb_kernel(tc, x, y_attn, w_gate, w_proj, out):
         grpp = ctx.enter_context(tc.tile_pool(name="grpp", bufs=NB_GRP))
         xgp = ctx.enter_context(tc.tile_pool(name="xgp", bufs=4))
         wcp = ctx.enter_context(tc.tile_pool(name="wcp", bufs=NB_C))
-        sigp = ctx.enter_context(tc.tile_pool(name="sigp", bufs=2))
+        sigp = ctx.enter_context(tc.tile_pool(name="sigp", bufs=NB_SIG))
         hgp = ctx.enter_context(tc.tile_pool(name="hgp", bufs=2))
         outp = ctx.enter_context(tc.tile_pool(name="outp", bufs=NB_OUT))
         warmp = ctx.enter_context(tc.tile_pool(name="warmp", bufs=1))
@@ -85,6 +94,13 @@ def tile_multiheadattention_pb_kernel(tc, x, y_attn, w_gate, w_proj, out):
 
         ident = const.tile([P, P], F32, name="ident")
         make_identity(nc, ident[:])
+
+        zeros = const.tile([P, M], BF16, name="zeros")
+        nc.gpsimd.memset(zeros[:], 0.0)
+
+        def warm(bank, n):
+            for i in range(n):
+                nc.tensor.matmul(out=bank, lhsT=zeros[:, 0:P], rhs=zeros[:], start=True, stop=True)
 
         x_sb = [keep.tile([P, C], BF16, name="x_sb%d" % mt) for mt in range(MT)]
         y_sb = [keep.tile([P, MT, 1024], BF16, name="y_sb%d" % h) for h in range(2)]
@@ -115,11 +131,14 @@ def tile_multiheadattention_pb_kernel(tc, x, y_attn, w_gate, w_proj, out):
         left = {}
 
         loads = []
+        for mt in range(MT):
+            if X_LOAD[mt] == 0:
+                loads.append(("x", mt))
         for n, pl in enumerate(plan):
             loads.append(("w",) + pl)
-            for h in range(2):
-                if n + 1 == X_LOAD[h]:
-                    loads += [("x", 2 * h), ("x", 2 * h + 1)]
+            for mt in range(MT):
+                if n + 1 == X_LOAD[mt]:
+                    loads.append(("x", mt))
             for h in range(2):
                 if n + 1 == Y_AFTER[h]:
                     loads.append(("y", h))
@@ -149,10 +168,19 @@ def tile_multiheadattention_pb_kernel(tc, x, y_attn, w_gate, w_proj, out):
                     raw = slots[sk][:, g % n, :, :]
                     raws[(stage, c0, g)] = (raw, sk)
                     src = (w_gate if stage == "g" else w_proj)[512 * g:512 * (g + 1), c0:c0 + w]
-                    nc.sync.dma_start(out=raw, in_=src.rearrange("(p j) c -> p j c", j=4))
+                    parts = w // CH if stage == "g" and g < SPLIT else 1
+                    pw = w // parts
+                    for q in range(parts):
+                        nc.sync.dma_start(
+                            out=raw[:, :, pw * q:pw * (q + 1)],
+                            in_=src[:, pw * q:pw * (q + 1)].rearrange("(p j) c -> p j c", j=4),
+                        )
                 loads.pop(0)
 
         load_more()
+        if WARM0:
+            wb = psum.tile([P, M], F32, name="bank")
+            warm(wb[:], WARM0)
 
         grps = {}
         cods = {}
@@ -183,6 +211,7 @@ def tile_multiheadattention_pb_kernel(tc, x, y_attn, w_gate, w_proj, out):
             xgs = []
             for g in range(NG):
                 ps = psum.tile([P, 2, 256], F32, name="bank")
+                warm(ps[:].rearrange("p u m -> p (u m)"), WARM_X[g])
                 for u in range(2):
                     for i in range(2):
                         nc.tensor.transpose(
@@ -224,6 +253,8 @@ def tile_multiheadattention_pb_kernel(tc, x, y_attn, w_gate, w_proj, out):
                     banks[(ch, b)] = psy.tile([P, w], F32, name="ybank")
                 elif g == 0:
                     banks[(ch, b)] = psum.tile([P, M if stage == "g" else w], F32, name="bank")
+                    if b == 0 and w == M:
+                        warm(banks[(ch, b)][:], WARM_C[ch])
                 if stage == "g":
                     nc.tensor.matmul_mx(
                         out=banks[(ch, b)][:],
@@ -265,16 +296,18 @@ def tile_multiheadattention_pb_kernel(tc, x, y_attn, w_gate, w_proj, out):
                 passes(ch, g)
                 if g == NG - 1:
                     if ch < NGC:
-                        later(now + LAG_SIG, ("sig", ch, 0))
-                        later(now + LAG_SIG + SIG_GAP, ("sig", ch, 1))
-                        later(now + LAG_MUL, ("mul", ch, 0))
-                        later(now + LAG_MUL + MUL_GAP, ("mul", ch, 1))
-                        later(now + LAG_MUL + MUL_GAP + LAG_HQ, ("hq", ch, 0))
+                        at = now + (LAG_SIG if ch < NGC - 1 else LAG_SIG_L)
+                        for j in range(4):
+                            later(at + SIG_AT[j], ("sig", ch, j))
+                        ml = LAG_MUL if ch < NGC - 1 else LAG_MUL_L
+                        for j in range(4):
+                            later(now + ml + MUL_AT[j], ("mul", ch, j))
+                        later(now + ml + MUL_AT[3] + LAG_HQ, ("hq", ch, 0))
                         if ch + 1 < NGC:
-                            later(now + LAG_MUL + MUL_GAP + 1, ("ytr", ch + 1, 0))
+                            later(now + ml + MUL_AT[3] + LAG_YTR, ("ytr", ch + 1, 0))
                     else:
-                        later(now + LAG_OUT, ("out", ch, 0))
-                        later(now + LAG_OUT + OUT_GAP, ("out", ch, 1))
+                        for j in range(4):
+                            later(now + LAG_OUT + OUT_AT[j], ("out", ch, j))
 
         def quantise(k, now):
             stage, key, c0, w, g, ch = steps[k]
@@ -293,9 +326,8 @@ def tile_multiheadattention_pb_kernel(tc, x, y_attn, w_gate, w_proj, out):
             if kind == "sig":
                 if part == 0:
                     sigs[ch] = sigp.tile([P, 4, M], F32, name="sig")
-                for j in (2 * part, 2 * part + 1):
-                    nc.scalar.activation(out=sigs[ch][:, j, :], in_=banks[(ch, j)][:], func=ACT.Sigmoid)
-                if part == 1:
+                nc.scalar.activation(out=sigs[ch][:, part, :], in_=banks[(ch, part)][:], func=ACT.Sigmoid)
+                if part == 3:
                     done.add(("sig", ch))
                     flush(now)
             elif kind == "ytr":
@@ -313,13 +345,16 @@ def tile_multiheadattention_pb_kernel(tc, x, y_attn, w_gate, w_proj, out):
             elif kind == "mul":
                 if part == 0:
                     hgs[ch] = hgp.tile([P, 4 * M], BF16, name="hg", align_bytes=64)
-                nc.vector.tensor_tensor(
-                    out=hgs[ch][:, 1024 * part:1024 * (part + 1)].rearrange("p (m u e) -> p m u e", u=2, e=2),
-                    in0=sigs[ch][:, :, 256 * part:256 * (part + 1)].rearrange("p (u e) m -> p m u e", e=2),
-                    in1=yps[(ch, part)][:].bitcast(BF16).rearrange("p u (m e) -> p m u e", e=2),
-                    op=ALU.mult,
-                )
-                if part == 1:
+                if part % MUL_W == MUL_W - 1:
+                    t0, t1 = P * (part + 1 - MUL_W), P * (part + 1)
+                    yp = yps[(ch, part // 2)][:].bitcast(BF16)
+                    nc.vector.tensor_tensor(
+                        out=hgs[ch][:, 4 * t0:4 * t1].rearrange("p (m u e) -> p m u e", u=2, e=2),
+                        in0=sigs[ch][:, :, t0:t1].rearrange("p (u e) m -> p m u e", e=2),
+                        in1=yp[:, :, 2 * (t0 % 256):2 * (t0 % 256) + 2 * (t1 - t0)].rearrange("p u (m e) -> p m u e", e=2),
+                        op=ALU.mult,
+                    )
+                if part == 3:
                     done.add(("mul", ch))
             elif kind == "hq":
                 nc.vector.quantize_mx(out=hc[:, ch, :].bitcast(FP8X4), scales=hs[:, ch, :], in_=hgs[ch][:])
@@ -328,14 +363,14 @@ def tile_multiheadattention_pb_kernel(tc, x, y_attn, w_gate, w_proj, out):
             elif kind == "out":
                 stage, lo, w = chunks[ch]
                 last = ch == len(chunks) - 1
-                for mt in (2 * part, 2 * part + 1):
+                for mt in (part,):
                     ob = outp.tile([P, w], F32, name="ob")
                     if mt in (LAST_V if last else OUT_V):
                         nc.vector.tensor_copy(out=ob[:], in_=banks[(ch, mt)][:])
                     else:
                         nc.scalar.copy(out=ob[:], in_=banks[(ch, mt)][:])
                     nc.sync.dma_start(out=of[P * mt:P * (mt + 1), lo:lo + w], in_=ob[:])
-                if part == 1:
+                if part == 3:
                     done.add(("out", ch))
                     flush(now)
 
@@ -344,10 +379,11 @@ def tile_multiheadattention_pb_kernel(tc, x, y_attn, w_gate, w_proj, out):
         k = 0
         while k <= NI or any(n >= k for n in todo):
             jobs = todo.get(k, [])
-            s_job = sum(1 for j in jobs if j[0] == "sig")
-            s_job += sum(1 for j in jobs if j[0] == "out") * (2 - len(OUT_V)) / 2
+            s_job = sum(1 for j in jobs if j[0] == "sig") / 2
+            s_job += sum(1 for j in jobs if j[0] == "out" and j[2] not in OUT_V) / 2
+            v_out = sum(1 for j in jobs if j[0] == "out" and j[2] in OUT_V) / 2
             s_job += sum(1 for h in range(2) if k == X_STEP[h]) * X_S
-            v_job = sum(1 for j in jobs if j[0] == "mul")
+            v_job = sum(1 for j in jobs if j[0] == "mul") / 2 + v_out
             for job in jobs:
                 if job[0] in ("sig", "out", "ytr", "mul"):
                     run_job(job, k)

@@ -333,12 +333,12 @@ def tile_multiheadattention_pb_kernel(tc, x, y_attn, w_gate, w_proj, out):
             elif kind == "ytr":
                 yw = y_sb[ch // 2][:, :, CH * (ch % 2):CH * (ch % 2 + 1)]
                 for half in range(2):
-                    yp = psy.tile([P, 2, 256], F32, name="ybank")
+                    yp = psy.tile([P, 256, 2], F32, name="ybank")
                     yps[(ch, half)] = yp
                     for u in range(2):
                         for i in range(2):
                             nc.tensor.transpose(
-                                yp[:, u, P * i:P * (i + 1)],
+                                yp[:, P * i:P * (i + 1), u],
                                 yw[:, 2 * half + i, :].bitcast(F32)[:, u::2],
                                 ident[:],
                             )
@@ -347,11 +347,11 @@ def tile_multiheadattention_pb_kernel(tc, x, y_attn, w_gate, w_proj, out):
                     hgs[ch] = hgp.tile([P, 4 * M], BF16, name="hg", align_bytes=64)
                 if part % MUL_W == MUL_W - 1:
                     t0, t1 = P * (part + 1 - MUL_W), P * (part + 1)
-                    yp = yps[(ch, part // 2)][:].bitcast(BF16)
+                    yp = yps[(ch, part // 2)][:].rearrange("p m u -> p (m u)").bitcast(BF16)
                     nc.vector.tensor_tensor(
-                        out=hgs[ch][:, 4 * t0:4 * t1].rearrange("p (m u e) -> p m u e", u=2, e=2),
-                        in0=sigs[ch][:, :, t0:t1].rearrange("p (u e) m -> p m u e", e=2),
-                        in1=yp[:, :, 2 * (t0 % 256):2 * (t0 % 256) + 2 * (t1 - t0)].rearrange("p u (m e) -> p m u e", e=2),
+                        out=hgs[ch][:, 4 * t0:4 * t1].rearrange("p (b m j) -> p b j m", m=4, j=4),
+                        in0=sigs[ch][:, :, t0:t1].rearrange("p j (b m) -> p b j m", m=4),
+                        in1=yp[:, 4 * (t0 % 256):4 * (t0 % 256) + 4 * (t1 - t0)].rearrange("p (b m j) -> p b j m", m=4, j=4),
                         op=ALU.mult,
                     )
                 if part == 3:

@@ -193,11 +193,11 @@ def tile_multiheadattention_pb_kernel(tc, x, y_attn, w_gate, w_proj, out):
             for eng, a, b in (("v", 0, cv), ("s", cv, w)):
                 if b > a:
                     if stage == "g":
-                        dst = grp[:].rearrange("p (t b m j) -> p b j m t", t=4, m=2, j=4)[:, a // 8:b // 8]
-                        src = raw[:, :, c0 + a:c0 + b].rearrange("p j (b m t) -> p b j m t", m=2, t=4)
+                        dst = grp[:].rearrange("p (t m a e) -> p m a t e", t=4, a=2, e=2)[:, a // 4:b // 4]
+                        src = raw[:, :, c0 + a:c0 + b].rearrange("p (a e) (m t) -> p m a t e", e=2, t=4)
                     else:
-                        dst = grp[:, 4 * a:4 * b].rearrange("p (c i t) -> p c t i", i=8, t=4)
-                        src = raw[:, :, c0 + a:c0 + b].rearrange("p t (c i) -> p c t i", i=8)
+                        dst = grp[:, 4 * a:4 * b].rearrange("p (c i a e) -> p c a i e", i=8, a=2, e=2)
+                        src = raw[:, :, c0 + a:c0 + b].rearrange("p (a e) (c i) -> p c a i e", e=2, i=8)
                     if eng == "v":
                         nc.vector.tensor_copy(out=dst, in_=src)
                     else:
@@ -210,19 +210,18 @@ def tile_multiheadattention_pb_kernel(tc, x, y_attn, w_gate, w_proj, out):
         def x_transposes(half):
             xgs = []
             for g in range(NG):
-                ps = psum.tile([P, 2, 256], F32, name="bank")
-                warm(ps[:].rearrange("p u m -> p (u m)"), WARM_X[g])
+                ps = psum.tile([P, 256, 2], F32, name="bank")
                 for u in range(2):
                     for i in range(2):
                         nc.tensor.transpose(
-                            ps[:, u, P * i:P * (i + 1)],
+                            ps[:, P * i:P * (i + 1), u],
                             x_sb[2 * half + i][:].bitcast(F32)[:, 256 * g + u:256 * (g + 1):2],
                             ident[:],
                         )
                 xg = xgp.tile([P, 1024], BF16, name="xg", align_bytes=64)
                 xgs.append(xg)
-                dst = xg[:].bitcast(F32).rearrange("p (m u) -> p m u", u=2)
-                src = ps[:].rearrange("p u m -> p m u")
+                dst = xg[:].bitcast(F32)
+                src = ps[:].rearrange("p m u -> p (m u)")
                 if g in X_ON_V:
                     nc.vector.tensor_copy(out=dst, in_=src)
                 else:

@@ -62,7 +62,7 @@ X_FIRST = 1
 X_S = 0
 OUT_V = ()
 Y0 = 6
-V_NONE = 256
+V_NONE = 272
 
 
 def tile_multiheadattention_pb_kernel(tc, x, y_attn, w_gate, w_proj, out):
@@ -348,9 +348,9 @@ def tile_multiheadattention_pb_kernel(tc, x, y_attn, w_gate, w_proj, out):
                     t0, t1 = P * (part + 1 - MUL_W), P * (part + 1)
                     yp = yps[(ch, part // 2)][:].rearrange("p m u -> p (m u)").bitcast(BF16)
                     nc.vector.tensor_tensor(
-                        out=hgs[ch][:, 4 * t0:4 * t1].rearrange("p (b m j) -> p b j m", m=4, j=4),
-                        in0=sigs[ch][:, :, t0:t1].rearrange("p j (b m) -> p b j m", m=4),
-                        in1=yp[:, 4 * (t0 % 256):4 * (t0 % 256) + 4 * (t1 - t0)].rearrange("p (b m j) -> p b j m", m=4, j=4),
+                        out=hgs[ch][:, 4 * t0:4 * t1].rearrange("p (b m j) -> p b j m", m=2, j=4),
+                        in0=sigs[ch][:, :, t0:t1].rearrange("p j (b m) -> p b j m", m=2),
+                        in1=yp[:, 4 * (t0 % 256):4 * (t0 % 256) + 4 * (t1 - t0)].rearrange("p (b m j) -> p b j m", m=2, j=4),
                         op=ALU.mult,
                     )
                 if part == 3:
@@ -396,7 +396,7 @@ def tile_multiheadattention_pb_kernel(tc, x, y_attn, w_gate, w_proj, out):
                     cols = V_FIRST[k]
                 if w < CH:
                     cols = cols * w // CH
-                cols = min(max(cols // 32 * 32, 0), w)
+                cols = min(max(cols // 16 * 16, 0), w)
                 regroup(k, cols)
             if 0 < k <= NI:
                 quantise(k - 1, k)

from contextlib import ExitStack

import concourse.mybir as mybir
from concourse.masks import make_identity

F32 = mybir.dt.float32
BF16 = mybir.dt.bfloat16
U32 = mybir.dt.uint32
U8 = mybir.dt.uint8
FP8X4 = mybir.dt.float8_e4m3fn_x4
ACT = mybir.ActivationFunctionType
ALU = mybir.AluOpType

P = 128
M = 512
C = 2048
NG = 4
CH = 512
MT = M // P

FLOPS = 2 * 2 * M * C * C

GATE_LOADS = ((0, 512), (512, 512), (1024, 512), (1536, 512))
PROJ_LOADS = ((0, 1024), (1024, 1024))
PROJ_CHUNKS = (((0, 512), (512, 512)), ((1024, 512), (1536, 256), (1792, 256)))
GATE_K_FIRST = (False,)*4
PROJ_K_FIRST = (0, 0)

Y_AFTER = (8,11)
RAW_KIB = 96

V_NONE, V_S_JOB, V_V_JOB = 256, 416, 96
LAG_SIG = 3
LAG_MUL = 5
LAG_HQ = 0
LAG_OUT = 5
LAST_V = (1, 3)

NSLOT = 5
NB_C = 12
X_ON_V = ()
SIG_AT = (0,0,0,0)
MUL_AT = (0,0,0,0)
OUT_AT = (0,0,0,0)
MUL_W = 2
LAG_YTR = 0
LAG_SIG_L = 2
LAG_MUL_L = 3
V_STEP = 192
V_FIRST = {}
X_GAP = 0
WARM0 = 0
WARM_X = (0,0,0,0)
WARM_C = (0,)*10
NB_SIG = 2
SPLIT = 1
NB_GRP = 5
NB_OUT = 8
X_LOAD = (1,1,3,3)
X_STEP = (1,3)
X_FIRST = 1
X_S = 0
OUT_V = ()
Y0 = 6
V_NONE = 272


def tile_multiheadattention_pb_kernel(tc, x, y_attn, w_gate, w_proj, out):
    nc = tc.nc
    xf = x.flatten_outer_dims()
    yf = y_attn.rearrange("b t h d -> (b t) (h d)")
    of = out.flatten_outer_dims()

    with ExitStack() as ctx:
        const = ctx.enter_context(tc.tile_pool(name="const", bufs=1))
        keep = ctx.enter_context(tc.tile_pool(name="keep", bufs=1))
        rawp = ctx.enter_context(tc.tile_pool(name="raw", bufs=NSLOT))
        grpp = ctx.enter_context(tc.tile_pool(name="grpp", bufs=NB_GRP))
        xgp = ctx.enter_context(tc.tile_pool(name="xgp", bufs=4))
        wcp = ctx.enter_context(tc.tile_pool(name="wcp", bufs=NB_C))
        sigp = ctx.enter_context(tc.tile_pool(name="sigp", bufs=NB_SIG))
        hgp = ctx.enter_context(tc.tile_pool(name="hgp", bufs=2))
        outp = ctx.enter_context(tc.tile_pool(name="outp", bufs=NB_OUT))
        warmp = ctx.enter_context(tc.tile_pool(name="warmp", bufs=1))
        psum = ctx.enter_context(tc.psum_pool(name="psum", bufs=6))
        psy = ctx.enter_context(tc.psum_pool(name="psy", bufs=2))

        ctx.enter_context(tc.manual_schedule())

        warm_in = warmp.tile([P, 1], F32, name="warm_in")
        warm_out = warmp.tile([P, 1], F32, name="warm_out")
        nc.vector.memset(warm_in[:], 0.0)
        nc.scalar.activation(out=warm_out[:], in_=warm_in[:], func=ACT.Sigmoid)

        ident = const.tile([P, P], F32, name="ident")
        make_identity(nc, ident[:])

        zeros = const.tile([P, M], BF16, name="zeros")
        nc.gpsimd.memset(zeros[:], 0.0)

        def warm(bank, n):
            for i in range(n):
                nc.tensor.matmul(out=bank, lhsT=zeros[:, 0:P], rhs=zeros[:], start=True, stop=True)

        x_sb = [keep.tile([P, C], BF16, name="x_sb%d" % mt) for mt in range(MT)]
        y_sb = [keep.tile([P, MT, 1024], BF16, name="y_sb%d" % h) for h in range(2)]
        xc = keep.tile([P, NG, M], U32, name="xc", align_bytes=64)
        xs = keep.tile([P, NG, M], U8, name="xs", align_bytes=64)
        hc = keep.tile([P, NG, M], U32, name="hc", align_bytes=64)
        hs = keep.tile([P, NG, M], U8, name="hs", align_bytes=64)

        steps = []
        plan = []
        chunks = []
        for stage, loads, kfirst in (("g", GATE_LOADS, GATE_K_FIRST), ("p", PROJ_LOADS, PROJ_K_FIRST)):
            for b, (c0, w) in enumerate(loads):
                parts = [(c, CH) for c in range(c0, c0 + w, CH)] if stage == "g" else PROJ_CHUNKS[b]
                n0 = len(chunks)
                chunks += [(stage, lo, pw) for lo, pw in parts]
                nk = len(parts) if kfirst[b] is True else int(kfirst[b])
                order = [(g, i) for g in range(NG) for i in range(nk)]
                order += [(g, i) for i in range(nk, len(parts)) for g in range(NG)]
                for g in range(NG):
                    plan.append((stage, c0, w, g))
                for g, i in order:
                    steps.append((stage, (stage, c0, g), parts[i][0] - c0, parts[i][1], g, n0 + i))
        NGC = sum(1 for ch in chunks if ch[0] == "g")
        NI = len(steps)

        raws = {}
        left = {}

        loads = []
        for mt in range(MT):
            if X_LOAD[mt] == 0:
                loads.append(("x", mt))
        for n, pl in enumerate(plan):
            loads.append(("w",) + pl)
            for mt in range(MT):
                if n + 1 == X_LOAD[mt]:
                    loads.append(("x", mt))
            for h in range(2):
                if n + 1 == Y_AFTER[h]:
                    loads.append(("y", h))
        room = [NSLOT]
        slots = {}

        def load_more():
            while loads:
                ld = loads[0]
                if ld[0] == "x":
                    nc.sync.dma_start(out=x_sb[ld[1]][:], in_=xf[P * ld[1]:P * (ld[1] + 1), :])
                elif ld[0] == "y":
                    nc.sync.dma_start(
                        out=y_sb[ld[1]][:],
                        in_=yf[:, 1024 * ld[1]:1024 * (ld[1] + 1)].rearrange("(t p) c -> p t c", p=P),
                    )
                else:
                    stage, c0, w, g = ld[1:]
                    n = 2048 // w
                    sk = (stage, c0, g // n)
                    if sk not in slots:
                        if room[0] == 0:
                            return
                        room[0] -= 1
                        slots[sk] = rawp.tile([P, n, 4, w], BF16, name="raw")
                        left[sk] = n * w
                    raw = slots[sk][:, g % n, :, :]
                    raws[(stage, c0, g)] = (raw, sk)
                    src = (w_gate if stage == "g" else w_proj)[512 * g:512 * (g + 1), c0:c0 + w]
                    parts = w // CH if stage == "g" and g < SPLIT else 1
                    pw = w // parts
                    for q in range(parts):
                        nc.sync.dma_start(
                            out=raw[:, :, pw * q:pw * (q + 1)],
                            in_=src[:, pw * q:pw * (q + 1)].rearrange("(p j) c -> p j c", j=4),
                        )
                loads.pop(0)

        load_more()
        if WARM0:
            wb = psum.tile([P, M], F32, name="bank")
            warm(wb[:], WARM0)

        grps = {}
        cods = {}

        def regroup(k, cv):
            stage, key, c0, w, g, ch = steps[k]
            grp = grpp.tile([P, 4 * w], BF16, name="grp", align_bytes=64)
            grps[k] = grp
            raw, sk = raws[key]
            for eng, a, b in (("v", 0, cv), ("s", cv, w)):
                if b > a:
                    if stage == "g":
                        dst = grp[:].rearrange("p (t m a e) -> p m a t e", t=4, a=2, e=2)[:, a // 4:b // 4]
                        src = raw[:, :, c0 + a:c0 + b].rearrange("p (a e) (m t) -> p m a t e", e=2, t=4)
                    else:
                        dst = grp[:, 4 * a:4 * b].rearrange("p (c i a e) -> p c a i e", i=8, a=2, e=2)
                        src = raw[:, :, c0 + a:c0 + b].rearrange("p (a e) (c i) -> p c a i e", e=2, i=8)
                    if eng == "v":
                        nc.vector.tensor_copy(out=dst, in_=src)
                    else:
                        nc.scalar.copy(out=dst, in_=src)
            left[sk] -= w
            if left[sk] == 0:
                room[0] += 1
            load_more()

        def x_transposes(half):
            xgs = []
            for g in range(NG):
                ps = psum.tile([P, 256, 2], F32, name="bank")
                for u in range(2):
                    for i in range(2):
                        nc.tensor.transpose(
                            ps[:, P * i:P * (i + 1), u],
                            x_sb[2 * half + i][:].bitcast(F32)[:, 256 * g + u:256 * (g + 1):2],
                            ident[:],
                        )
                xg = xgp.tile([P, 1024], BF16, name="xg", align_bytes=64)
                xgs.append(xg)
                dst = xg[:].bitcast(F32)
                src = ps[:].rearrange("p m u -> p (m u)")
                if g in X_ON_V:
                    nc.vector.tensor_copy(out=dst, in_=src)
                else:
                    nc.scalar.copy(out=dst, in_=src)
            return xgs

        def x_quantise(half, xgs):
            for g in range(NG):
                nc.vector.quantize_mx(
                    out=xc[:, g, 256 * half:256 * (half + 1)].bitcast(FP8X4),
                    scales=xs[:, g, 256 * half:256 * (half + 1)],
                    in_=xgs[g][:],
                )

        banks = {}
        queue = [(ch, g) for ch in range(len(chunks)) for g in range(NG)]
        done = set()
        todo = {}

        def later(k, what):
            todo.setdefault(k, []).append(what)

        def passes(ch, g):
            stage, lo, w = chunks[ch]
            wcod, wsca = cods[(ch, g)]
            for b in range(4):
                if g == 0 and stage == "p" and b == 3:
                    banks[(ch, b)] = psy.tile([P, w], F32, name="ybank")
                elif g == 0:
                    banks[(ch, b)] = psum.tile([P, M if stage == "g" else w], F32, name="bank")
                    if b == 0 and w == M:
                        warm(banks[(ch, b)][:], WARM_C[ch])
                if stage == "g":
                    nc.tensor.matmul_mx(
                        out=banks[(ch, b)][:],
                        lhsT=wcod[:, P * b:P * (b + 1)].bitcast(FP8X4),
                        lhsT_scale=wsca[:, P * b:P * (b + 1)],
                        rhs=xc[:, g, :].bitcast(FP8X4),
                        rhs_scale=xs[:, g, :],
                        start=(g == 0),
                        stop=(g == NG - 1),
                    )
                else:
                    nc.tensor.matmul_mx(
                        out=banks[(ch, b)][:],
                        lhsT=hc[:, g, P * b:P * (b + 1)].bitcast(FP8X4),
                        lhsT_scale=hs[:, g, P * b:P * (b + 1)],
                        rhs=wcod[:].bitcast(FP8X4),
                        rhs_scale=wsca[:],
                        start=(g == 0),
                        stop=(g == NG - 1),
                    )

        def ready(ch, g):
            if (ch, g) not in cods or "x" not in done:
                return False
            if ch >= NGC and ("hq", g) not in done:
                return False
            if g == 0 and ch > 0:
                if ch == NGC:
                    return ("sig", NGC - 1) in done and ("mul", NGC - 1) in done
                if ch < NGC:
                    return ("sig", ch - 1) in done
                if ch >= NGC + 2:
                    return ("out", ch - 2) in done
            return True

        def flush(now):
            while queue and ready(*queue[0]):
                ch, g = queue.pop(0)
                passes(ch, g)
                if g == NG - 1:
                    if ch < NGC:
                        at = now + (LAG_SIG if ch < NGC - 1 else LAG_SIG_L)
                        for j in range(4):
                            later(at + SIG_AT[j], ("sig", ch, j))
                        ml = LAG_MUL if ch < NGC - 1 else LAG_MUL_L
                        for j in range(4):
                            later(now + ml + MUL_AT[j], ("mul", ch, j))
                        later(now + ml + MUL_AT[3] + LAG_HQ, ("hq", ch, 0))
                        if ch + 1 < NGC:
                            later(now + ml + MUL_AT[3] + LAG_YTR, ("ytr", ch + 1, 0))
                    else:
                        for j in range(4):
                            later(now + LAG_OUT + OUT_AT[j], ("out", ch, j))

        def quantise(k, now):
            stage, key, c0, w, g, ch = steps[k]
            wcod = wcp.tile([P, w], U32, name="wcod", align_bytes=64)
            wsca = wcp.tile([P, w], U8, name="wsca", align_bytes=64)
            cods[(ch, g)] = (wcod, wsca)
            nc.vector.quantize_mx(out=wcod[:].bitcast(FP8X4), scales=wsca[:], in_=grps[k][:])
            flush(now)

        sigs = {}
        yps = {}
        hgs = {}

        def run_job(job, now):
            kind, ch, part = job
            if kind == "sig":
                if part == 0:
                    sigs[ch] = sigp.tile([P, 4, M], F32, name="sig")
                nc.scalar.activation(out=sigs[ch][:, part, :], in_=banks[(ch, part)][:], func=ACT.Sigmoid)
                if part == 3:
                    done.add(("sig", ch))
                    flush(now)
            elif kind == "ytr":
                yw = y_sb[ch // 2][:, :, CH * (ch % 2):CH * (ch % 2 + 1)]
                for half in range(2):
                    yp = psy.tile([P, 256, 2], F32, name="ybank")
                    yps[(ch, half)] = yp
                    for u in range(2):
                        for i in range(2):
                            nc.tensor.transpose(
                                yp[:, P * i:P * (i + 1), u],
                                yw[:, 2 * half + i, :].bitcast(F32)[:, u::2],
                                ident[:],
                            )
            elif kind == "mul":
                if part == 0:
                    hgs[ch] = hgp.tile([P, 4 * M], BF16, name="hg", align_bytes=64)
                if part % MUL_W == MUL_W - 1:
                    t0, t1 = P * (part + 1 - MUL_W), P * (part + 1)
                    yp = yps[(ch, part // 2)][:].rearrange("p m u -> p (m u)").bitcast(BF16)
                    nc.vector.tensor_tensor(
                        out=hgs[ch][:, 4 * t0:4 * t1].rearrange("p (b m j) -> p b j m", m=2, j=4),
                        in0=sigs[ch][:, :, t0:t1].rearrange("p j (b m) -> p b j m", m=2),
                        in1=yp[:, 4 * (t0 % 256):4 * (t0 % 256) + 4 * (t1 - t0)].rearrange("p (b m j) -> p b j m", m=2, j=4),
                        op=ALU.mult,
                    )
                if part == 3:
                    done.add(("mul", ch))
            elif kind == "hq":
                nc.vector.quantize_mx(out=hc[:, ch, :].bitcast(FP8X4), scales=hs[:, ch, :], in_=hgs[ch][:])
                done.add(("hq", ch))
                flush(now)
            elif kind == "out":
                stage, lo, w = chunks[ch]
                last = ch == len(chunks) - 1
                for mt in (part,):
                    ob = outp.tile([P, w], F32, name="ob")
                    if mt in (LAST_V if last else OUT_V):
                        nc.vector.tensor_copy(out=ob[:], in_=banks[(ch, mt)][:])
                    else:
                        nc.scalar.copy(out=ob[:], in_=banks[(ch, mt)][:])
                    nc.sync.dma_start(out=of[P * mt:P * (mt + 1), lo:lo + w], in_=ob[:])
                if part == 3:
                    done.add(("out", ch))
                    flush(now)

        later(Y0, ("ytr", 0, 0))
        xgs = {}
        k = 0
        while k <= NI or any(n >= k for n in todo):
            jobs = todo.get(k, [])
            s_job = sum(1 for j in jobs if j[0] == "sig") / 2
            s_job += sum(1 for j in jobs if j[0] == "out" and j[2] not in OUT_V) / 2
            v_out = sum(1 for j in jobs if j[0] == "out" and j[2] in OUT_V) / 2
            s_job += sum(1 for h in range(2) if k == X_STEP[h]) * X_S
            v_job = sum(1 for j in jobs if j[0] == "mul") / 2 + v_out
            for job in jobs:
                if job[0] in ("sig", "out", "ytr", "mul"):
                    run_job(job, k)
            for h in range(2):
                if k == X_STEP[h] and X_FIRST:
                    xgs[h] = x_transposes(h)
            if k < NI:
                w = steps[k][3]
                cols = int(V_NONE + V_STEP * (s_job - v_job))
                if k in V_FIRST:
                    cols = V_FIRST[k]
                if w < CH:
                    cols = cols * w // CH
                cols = min(max(cols // 16 * 16, 0), w)
                regroup(k, cols)
            if 0 < k <= NI:
                quantise(k - 1, k)
            for h in range(2):
                if k == X_STEP[h] and not X_FIRST:
                    xgs[h] = x_transposes(h)
            for job in todo.get(k, []):
                if job[0] == "hq":
                    run_job(job, k)
            for h in range(2):
                if k == X_STEP[h] + X_GAP:
                    x_quantise(h, xgs[h])
                    if h == 1:
                        done.add("x")
                        flush(k)
            k += 1
        assert not queue
